import numpy as np
import ml_dtypes


def mxq(x, axis, fmt="e4m3"):
    dtype, down = {"e4m3": (ml_dtypes.float8_e4m3fn, 7), "e5m2": (ml_dtypes.float8_e5m2, 14)}[fmt]
    v = np.moveaxis(np.asarray(x, np.float32).astype(ml_dtypes.bfloat16).astype(np.float64), axis, -1)
    blocks = v.reshape(v.shape[:-1] + (-1, 32))
    amax = np.abs(blocks).max(-1, keepdims=True)
    byte = np.maximum(np.where(amax > 0, np.frexp(amax)[1] - 1 + 127, 0) - down, 1)
    scale = np.exp2(byte - 127.0)
    codes = (blocks / scale).astype(np.float32).astype(dtype).astype(np.float64)
    return np.moveaxis((codes * scale).reshape(v.shape), -1, axis)


WIDE = False


def mx_kscale(k):
    if not WIDE:
        return np.ones(k)
    levels = np.array([10, -10, 5, -5, 0])
    a = np.random.permutation(np.resize(levels, k // 512 * 4)).reshape(k // 512, 4)
    idx = np.arange(k)
    return np.exp2(a[idx // 512, idx % 128 // 32])


BF16 = ml_dtypes.bfloat16


def bf(x):
    return np.asarray(x, np.float32).astype(BF16)


def f64(x):
    return np.asarray(x).astype(np.float64)


E2M1 = np.array([0.0, 0.5, 1.0, 1.5, 2.0, 3.0, 4.0, 6.0, -0.0, -0.5, -1.0, -1.5, -2.0, -3.0, -4.0, -6.0])


def pack_weight(w, fmt):
    k, n = w.shape
    w = f64(bf(w)).reshape(k // 32, 32, n)
    amax = np.abs(w).max(1)
    if fmt == "e4m3":
        byte = np.frexp(amax)[1] - 1 + 127 - 7
    else:
        mant, ex = np.frexp(amax / 6.0)
        byte = np.where(mant > 0.5, ex, ex - 1) + 127
    byte = np.clip(np.where(amax > 0, byte, 1), 1, 254)
    scaled = (w * np.exp2(127.0 - byte)[:, None, :]).reshape(k, n).astype(np.float32)
    by_word = np.ascontiguousarray(scaled.reshape(k // 512, 128, 4, n).transpose(0, 1, 3, 2))
    if fmt == "e4m3":
        words = by_word.astype(ml_dtypes.float8_e4m3fn).view(np.uint8)
    else:
        c = by_word.astype(ml_dtypes.float4_e2m1fn).view(np.uint8) & 0xF
        words = c[..., 0::2] | (c[..., 1::2] << 4)
    return np.ascontiguousarray(words), np.ascontiguousarray(byte.astype(np.uint8).reshape(k // 512, 16, n))


def unpack_weight(words, scales, fmt):
    g, p, n, _ = words.shape
    if fmt == "e4m3":
        vals = np.ascontiguousarray(words).view(ml_dtypes.float8_e4m3fn).astype(np.float64)
    else:
        nib = np.empty((g, p, n, 4), np.uint8)
        nib[..., 0::2] = words & 0xF
        nib[..., 1::2] = words >> 4
        vals = E2M1[nib]
    vals = vals * np.repeat(np.exp2(scales.astype(np.float64) - 127.0), 8, axis=1)[..., None]
    return vals.transpose(0, 1, 3, 2).reshape(g * 512, n)

def pack4(w):
    words, scales = pack_weight(w, "e2m1")
    return words.reshape(words.shape[0], 128, -1), scales


def unpack4(words, scales):
    return unpack_weight(words.reshape(words.shape[0], 128, -1, 2), scales, "e2m1")


B, F, H, E = 4096, 8, 512, 256


def setup_inputs():
    t = mx_kscale(H)
    x = bf(np.random.standard_normal((B, F)))
    w1 = bf(np.random.uniform(-1.0, 1.0, (F, H)) * t)
    b1 = bf(np.random.uniform(-1.0, 1.0, (F, H)) * t)
    w2 = np.random.standard_normal((F, H, E)) * 1.5 / np.sqrt(H) / t[None, :, None]
    w2_words, w2_scales = pack4(w2.reshape(-1, E))
    b2 = bf(np.random.standard_normal((F, E)) * 0.3)
    return {"x": x,
            "w1": w1,
            "b1": b1,
            "w2_words": w2_words,
            "w2_scales": w2_scales,
            "b2": b2}


def reference(x, w1, b1, w2_words, w2_scales, b2):
    h = np.maximum(f64(x)[:, :, None] * f64(w1)[None] + f64(b1)[None], 0.0)
    hq = mxq(h, 2, "e4m3")
    out = (hq.transpose(1, 0, 2) @ unpack4(w2_words, w2_scales).reshape(F, H, E)).transpose(1, 0, 2) + f64(b2)[None]
    return out.reshape(x.shape[0], F * E)

@@ -1,0 +1,165 @@
+from contextlib import ExitStack
+
+import concourse.mybir as mybir
+from concourse.masks import make_identity
+
+BF16 = mybir.dt.bfloat16
+F32 = mybir.dt.float32
+I32 = mybir.dt.int32
+U32 = mybir.dt.uint32
+U8 = mybir.dt.uint8
+FP8X4 = mybir.dt.float8_e4m3fn_x4
+FP4X4 = mybir.dt.float4_e2m1fn_x4
+
+P = 128
+PACK = 4
+BATCH, FEATURES, HIDDEN, EMBED = 4096, 8, 512, 256
+BATCH_TILES = BATCH // P
+UNIT_TILES = 8
+UNIT_COLS = UNIT_TILES * P
+UNITS = (BATCH_TILES // UNIT_TILES) * FEATURES
+BANK_TILES = 2
+RUN = 4
+
+FLOPS = 2 * BATCH * FEATURES * HIDDEN * EMBED
+
+
+def tile_densefeaturenumericembedding_t_e_kernel(tc, x, w1, b1, w2_words, w2_scales, b2, out):
+    nc = tc.nc
+    relu = mybir.ActivationFunctionType.Relu
+    mult = mybir.AluOpType.mult
+    add = mybir.AluOpType.add
+    out_rows = out.rearrange("(n c) w -> n c w", c=BATCH_TILES)
+
+    with ExitStack() as stack:
+        stack.enter_context(tc.manual_schedule())
+        const = stack.enter_context(tc.tile_pool(name="const", bufs=1))
+        x_pool = stack.enter_context(tc.tile_pool(name="x_pool", bufs=3))
+        z_pool = stack.enter_context(tc.tile_pool(name="z_pool", bufs=3))
+        h_pool = stack.enter_context(tc.tile_pool(name="h_pool", bufs=3))
+        q_pool = stack.enter_context(tc.tile_pool(name="q_pool", bufs=2))
+        o_pool = stack.enter_context(tc.tile_pool(name="o_pool", bufs=4))
+        x_banks = stack.enter_context(tc.psum_pool(name="x_banks", bufs=2))
+        acc_banks = stack.enter_context(tc.psum_pool(name="acc_banks", bufs=6))
+
+        x_sb = const.tile([P, BATCH_TILES * FEATURES], BF16)
+        nc.sync.dma_start(out=x_sb[:], in_=x.rearrange("(n c) f -> n (c f)", c=BATCH_TILES))
+        w1_bf = const.tile([P, FEATURES, PACK], BF16)
+        nc.sync.dma_start(out=w1_bf[:], in_=w1.rearrange("f (p t) -> p f t", t=PACK))
+        b1_bf = const.tile([P, FEATURES, PACK], BF16)
+        nc.sync.dma_start(out=b1_bf[:], in_=b1.rearrange("f (p t) -> p f t", t=PACK))
+        w2_codes = const.tile([P, FEATURES, 2 * EMBED], U8, align_bytes=64)
+        nc.sync.dma_start(out=w2_codes[:].bitcast(I32), in_=w2_words.bitcast(I32).rearrange("g p n -> p g n"))
+        w2_planes = const.tile([P, FEATURES, EMBED], U8, align_bytes=64)
+        nc.vector.memset(w2_planes[:].rearrange("p g n -> p (g n)").bitcast(I32), 0)
+        for quad in range(4):
+            nc.sync.dma_start(
+                out=w2_planes[32 * quad : 32 * quad + 4, :, :].bitcast(I32),
+                in_=w2_scales.bitcast(I32)[:, 4 * quad : 4 * quad + 4, :].rearrange("g q n -> q g n"),
+            )
+        b2_all = const.tile([P, FEATURES * EMBED], BF16)
+        nc.sync.dma_start(out=b2_all[:], in_=b2.rearrange("f e -> (f e)").partition_broadcast(P))
+
+        ident = const.tile([P, P], BF16)
+        make_identity(nc, ident[:])
+        w1_col = const.tile([P, FEATURES * PACK], F32)
+        nc.vector.tensor_copy(out=w1_col[:], in_=w1_bf[:].rearrange("p f t -> p (f t)"))
+        b1_col = const.tile([P, FEATURES * PACK], F32)
+        nc.vector.tensor_copy(out=b1_col[:], in_=b1_bf[:].rearrange("p f t -> p (f t)"))
+
+        live = {}
+
+        def first_tile(u):
+            return (u // FEATURES) * UNIT_TILES
+
+        def feature(u):
+            return u % FEATURES
+
+        def spread_on_tensor(u):
+            x_bank = x_banks.tile([P, UNIT_COLS], BF16)
+            for i in range(UNIT_TILES):
+                col = (first_tile(u) + i) * FEATURES + feature(u)
+                nc.tensor.transpose(
+                    x_bank[:, i * P : (i + 1) * P], x_sb[:, col : col + 1].to_broadcast([P, P]), ident[:]
+                )
+            live["x_bank", u] = x_bank
+
+        def spread_copy(u):
+            x_all = x_pool.tile([P, UNIT_COLS], BF16)
+            nc.scalar.copy(out=x_all[:], in_=live["x_bank", u][:])
+            live["x_all", u] = x_all
+
+        def affine(u):
+            z = z_pool.tile([P, PACK, UNIT_COLS], BF16)
+            for t in range(PACK):
+                s = feature(u) * PACK + t
+                nc.vector.tensor_scalar(
+                    out=z[:, t, :],
+                    in0=live["x_all", u][:],
+                    scalar1=w1_col[:, s : s + 1],
+                    scalar2=b1_col[:, s : s + 1],
+                    op0=mult,
+                    op1=add,
+                )
+            live["z", u] = z
+
+        def regroup(u):
+            h = h_pool.tile([P, UNIT_COLS, PACK], BF16, align_bytes=64)
+            nc.scalar.activation(
+                out=h[:].rearrange("p (c i) t -> p c t i", i=RUN),
+                in_=live["z", u][:].rearrange("p t (c i) -> p c t i", i=RUN),
+                func=relu,
+            )
+            live["h", u] = h
+
+        def quantise(u):
+            codes = q_pool.tile([P, UNIT_COLS], U32, align_bytes=64)
+            scales = q_pool.tile([P, UNIT_COLS], U8, align_bytes=64)
+            nc.vector.quantize_mx(
+                out=codes[:].bitcast(FP8X4), scales=scales[:], in_=live["h", u][:].rearrange("p b t -> p (b t)")
+            )
+            live["codes", u] = codes
+            live["scales", u] = scales
+
+        def multiply(u):
+            f = feature(u)
+            for k in range(UNIT_TILES // BANK_TILES):
+                acc = acc_banks.tile([P, BANK_TILES, EMBED], F32)
+                for s in range(BANK_TILES):
+                    cols = slice((k * BANK_TILES + s) * P, (k * BANK_TILES + s + 1) * P)
+                    nc.tensor.matmul_mx(
+                        out=acc[:, s, :],
+                        lhsT=live["codes", u][:, cols].bitcast(FP8X4),
+                        lhsT_scale=live["scales", u][:, cols],
+                        rhs=w2_codes[:, f, :].bitcast(FP4X4),
+                        rhs_scale=w2_planes[:, f, :],
+                        start=True,
+                        stop=True,
+                    )
+                live["acc", u, k] = acc
+
+        def bias_and_store(u):
+            f = feature(u)
+            o = o_pool.tile([P, UNIT_TILES, EMBED], F32)
+            b2_f = b2_all[:, f * EMBED : (f + 1) * EMBED].unsqueeze(1).to_broadcast([P, BANK_TILES, EMBED])
+            for k in range(UNIT_TILES // BANK_TILES):
+                nc.vector.tensor_tensor(
+                    out=o[:, k * BANK_TILES : (k + 1) * BANK_TILES, :], in0=live["acc", u, k][:], in1=b2_f, op=add
+                )
+            c0 = first_tile(u)
+            nc.sync.dma_start(out=out_rows[:, c0 : c0 + UNIT_TILES, f * EMBED : (f + 1) * EMBED], in_=o[:])
+
+        for r in range(-3, UNITS):
+            if 0 <= r + 3 < UNITS:
+                spread_on_tensor(r + 3)
+            if 0 <= r:
+                quantise(r)
+                multiply(r)
+            if 0 <= r + 1 < UNITS:
+                regroup(r + 1)
+            if 0 <= r + 3 < UNITS:
+                spread_copy(r + 3)
+            if 0 <= r + 2 < UNITS:
+                affine(r + 2)
+            if 0 <= r:
+                bias_and_store(r)

@@ -20,6 +20,8 @@ UNIT_COLS = UNIT_TILES * P
 UNITS = (BATCH_TILES // UNIT_TILES) * FEATURES
 BANK_TILES = 2
 RUN = 4
+VECTOR_COLS = 64
+SCALAR_COLS = UNIT_COLS - VECTOR_COLS
 
 FLOPS = 2 * BATCH * FEATURES * HIDDEN * EMBED
 
@@ -103,14 +105,21 @@ def tile_densefeaturenumericembedding_t_e_kernel(tc, x, w1, b1, w2_words, w2_sca
                 )
             live["z", u] = z
 
-        def regroup(u):
+        def regroup_on_scalar(u):
             h = h_pool.tile([P, UNIT_COLS, PACK], BF16, align_bytes=64)
             nc.scalar.activation(
-                out=h[:].rearrange("p (c i) t -> p c t i", i=RUN),
-                in_=live["z", u][:].rearrange("p t (c i) -> p c t i", i=RUN),
+                out=h[:, :SCALAR_COLS, :].rearrange("p (c i) t -> p c t i", i=RUN),
+                in_=live["z", u][:, :, :SCALAR_COLS].rearrange("p t (c i) -> p c t i", i=RUN),
                 func=relu,
             )
             live["h", u] = h
+
+        def regroup_on_vector(u):
+            nc.vector.tensor_scalar_max(
+                out=live["h", u][:, SCALAR_COLS:, :].rearrange("p (c i) t -> p c t i", i=RUN),
+                in0=live["z", u][:, :, SCALAR_COLS:].rearrange("p t (c i) -> p c t i", i=RUN),
+                scalar1=0.0,
+            )
 
         def quantise(u):
             codes = q_pool.tile([P, UNIT_COLS], U32, align_bytes=64)
@@ -156,7 +165,8 @@ def tile_densefeaturenumericembedding_t_e_kernel(tc, x, w1, b1, w2_words, w2_sca
                 quantise(r)
                 multiply(r)
             if 0 <= r + 1 < UNITS:
-                regroup(r + 1)
+                regroup_on_scalar(r + 1)
+                regroup_on_vector(r + 1)
             if 0 <= r + 3 < UNITS:
                 spread_copy(r + 3)
             if 0 <= r + 2 < UNITS:

@@ -20,8 +20,9 @@ UNIT_COLS = UNIT_TILES * P
 UNITS = (BATCH_TILES // UNIT_TILES) * FEATURES
 BANK_TILES = 2
 RUN = 4
-VECTOR_COLS = 64
-SCALAR_COLS = UNIT_COLS - VECTOR_COLS
+GPSIMD_COLS = 160
+SCALAR_COLS = UNIT_COLS - GPSIMD_COLS
+FLOAT32_MAX = 3.4028234663852886e38
 
 FLOPS = 2 * BATCH * FEATURES * HIDDEN * EMBED
 
@@ -114,11 +115,14 @@ def tile_densefeaturenumericembedding_t_e_kernel(tc, x, w1, b1, w2_words, w2_sca
             )
             live["h", u] = h
 
-        def regroup_on_vector(u):
-            nc.vector.tensor_scalar_max(
-                out=live["h", u][:, SCALAR_COLS:, :].rearrange("p (c i) t -> p c t i", i=RUN),
-                in0=live["z", u][:, :, SCALAR_COLS:].rearrange("p t (c i) -> p c t i", i=RUN),
-                scalar1=0.0,
+        def regroup_on_gpsimd(u):
+            nc.gpsimd.tensor_scalar(
+                out=live["h", u][:, SCALAR_COLS:, :],
+                in0=live["z", u][:, :, SCALAR_COLS:].rearrange("p t b -> p b t"),
+                scalar1=FLOAT32_MAX,
+                scalar2=0.0,
+                op0=mybir.AluOpType.min,
+                op1=mybir.AluOpType.max,
             )
 
         def quantise(u):
@@ -166,7 +170,7 @@ def tile_densefeaturenumericembedding_t_e_kernel(tc, x, w1, b1, w2_words, w2_sca
                 multiply(r)
             if 0 <= r + 1 < UNITS:
                 regroup_on_scalar(r + 1)
-                regroup_on_vector(r + 1)
+                regroup_on_gpsimd(r + 1)
             if 0 <= r + 3 < UNITS:
                 spread_copy(r + 3)
             if 0 <= r + 2 < UNITS:

@@ -162,10 +162,10 @@ def tile_densefeaturenumericembedding_t_e_kernel(tc, x, w1, b1, w2_words, w2_sca
             c0 = first_tile(u)
             nc.sync.dma_start(out=out_rows[:, c0 : c0 + UNIT_TILES, f * EMBED : (f + 1) * EMBED], in_=o[:])
 
-        for r in range(-3, UNITS):
+        for r in range(-3, UNITS + 1):
             if 0 <= r + 3 < UNITS:
                 spread_on_tensor(r + 3)
-            if 0 <= r:
+            if 0 <= r < UNITS:
                 quantise(r)
                 multiply(r)
             if 0 <= r + 1 < UNITS:
@@ -175,5 +175,5 @@ def tile_densefeaturenumericembedding_t_e_kernel(tc, x, w1, b1, w2_words, w2_sca
                 spread_copy(r + 3)
             if 0 <= r + 2 < UNITS:
                 affine(r + 2)
-            if 0 <= r:
-                bias_and_store(r)
+            if 0 <= r - 1:
+                bias_and_store(r - 1)

@@ -20,7 +20,7 @@ UNIT_COLS = UNIT_TILES * P
 UNITS = (BATCH_TILES // UNIT_TILES) * FEATURES
 BANK_TILES = 2
 RUN = 4
-GPSIMD_COLS = 160
+GPSIMD_COLS = 224
 SCALAR_COLS = UNIT_COLS - GPSIMD_COLS
 FLOAT32_MAX = 3.4028234663852886e38
 

@@ -18,6 +18,8 @@ BATCH_TILES = BATCH // P
 UNIT_TILES = 8
 UNIT_COLS = UNIT_TILES * P
 UNITS = (BATCH_TILES // UNIT_TILES) * FEATURES
+PARK_ROW = BATCH_TILES - FEATURES
+SPREAD_UNITS = 4
 BANK_TILES = 2
 RUN = 4
 GPSIMD_COLS = 224
@@ -78,6 +80,40 @@ def tile_densefeaturenumericembedding_t_e_kernel(tc, x, w1, b1, w2_words, w2_sca
         def feature(u):
             return u % FEATURES
 
+        x_by_feature = const.tile([P, FEATURES * BATCH_TILES], BF16)
+        nc.gpsimd.tensor_copy(
+            out=x_by_feature[:].rearrange("n (f c) -> n f c", f=FEATURES),
+            in_=x_sb[:].rearrange("n (c f) -> n f c", f=FEATURES),
+        )
+        x_turned = const.tile([P, 2 * P], BF16)
+        x_feat = const.tile([P, FEATURES, BATCH], BF16)
+
+        def turn_on_tensor():
+            x_bank = x_banks.tile([P, UNIT_COLS], BF16)
+            for half in range(2):
+                nc.tensor.transpose(
+                    x_bank[:, half * P : (half + 1) * P], x_by_feature[:, half * P : (half + 1) * P], ident[:]
+                )
+            live["turned"] = x_bank
+
+        def park():
+            nc.scalar.copy(out=x_turned[:], in_=live["turned"][:, : 2 * P])
+            pieces = out[PARK_ROW : PARK_ROW + FEATURES, :].rearrange("f (c w) -> (f c) w", c=BATCH_TILES)
+            for half in range(2):
+                nc.sync.dma_start(
+                    out=pieces[half * P : (half + 1) * P, :], in_=x_turned[:, half * P : (half + 1) * P].bitcast(F32)
+                )
+
+        def fetch(f):
+            row = out[PARK_ROW + f : PARK_ROW + f + 1, :].rearrange("r w -> (r w)")
+            nc.sync.dma_start(out=x_feat[:, f, :].bitcast(F32), in_=row.partition_broadcast(P))
+
+        def x_of(u):
+            if u < SPREAD_UNITS:
+                return live["x_all", u][:]
+            first = first_tile(u) * P
+            return x_feat[:, feature(u), first : first + UNIT_COLS]
+
         def spread_on_tensor(u):
             x_bank = x_banks.tile([P, UNIT_COLS], BF16)
             for i in range(UNIT_TILES):
@@ -98,7 +134,7 @@ def tile_densefeaturenumericembedding_t_e_kernel(tc, x, w1, b1, w2_words, w2_sca
                 s = feature(u) * PACK + t
                 nc.vector.tensor_scalar(
                     out=z[:, t, :],
-                    in0=live["x_all", u][:],
+                    in0=x_of(u),
                     scalar1=w1_col[:, s : s + 1],
                     scalar2=b1_col[:, s : s + 1],
                     op0=mult,
@@ -163,16 +199,22 @@ def tile_densefeaturenumericembedding_t_e_kernel(tc, x, w1, b1, w2_words, w2_sca
             nc.sync.dma_start(out=out_rows[:, c0 : c0 + UNIT_TILES, f * EMBED : (f + 1) * EMBED], in_=o[:])
 
         for r in range(-3, UNITS + 1):
-            if 0 <= r + 3 < UNITS:
+            if 0 <= r + 3 < SPREAD_UNITS:
                 spread_on_tensor(r + 3)
+            if r == -3:
+                turn_on_tensor()
             if 0 <= r < UNITS:
                 quantise(r)
                 multiply(r)
             if 0 <= r + 1 < UNITS:
                 regroup_on_scalar(r + 1)
                 regroup_on_gpsimd(r + 1)
-            if 0 <= r + 3 < UNITS:
+            if 0 <= r + 3 < SPREAD_UNITS:
                 spread_copy(r + 3)
+            if r == -3:
+                park()
+            if SPREAD_UNITS <= r + 7 < SPREAD_UNITS + FEATURES:
+                fetch(feature(r + 7))
             if 0 <= r + 2 < UNITS:
                 affine(r + 2)
             if 0 <= r - 1:

@@ -128,19 +128,32 @@ def tile_densefeaturenumericembedding_t_e_kernel(tc, x, w1, b1, w2_words, w2_sca
             nc.scalar.copy(out=x_all[:], in_=live["x_bank", u][:])
             live["x_all", u] = x_all
 
-        def affine(u):
+        def affine_on_scalar(u):
             z = z_pool.tile([P, PACK, UNIT_COLS], BF16)
+            live["z", u] = z
+            if u < SPREAD_UNITS:
+                return
+            s = feature(u) * PACK + PACK - 1
+            nc.scalar.activation(
+                out=z[:, PACK - 1, :SCALAR_COLS],
+                in_=x_of(u)[:, :SCALAR_COLS],
+                func=relu,
+                scale=w1_col[:, s : s + 1],
+                bias=b1_col[:, s : s + 1],
+            )
+
+        def affine(u):
             for t in range(PACK):
                 s = feature(u) * PACK + t
+                first = SCALAR_COLS if t == PACK - 1 and u >= SPREAD_UNITS else 0
                 nc.vector.tensor_scalar(
-                    out=z[:, t, :],
-                    in0=x_of(u),
+                    out=live["z", u][:, t, first:],
+                    in0=x_of(u)[:, first:],
                     scalar1=w1_col[:, s : s + 1],
                     scalar2=b1_col[:, s : s + 1],
                     op0=mult,
                     op1=add,
                 )
-            live["z", u] = z
 
         def regroup_on_scalar(u):
             h = h_pool.tile([P, UNIT_COLS, PACK], BF16, align_bytes=64)
@@ -216,6 +229,7 @@ def tile_densefeaturenumericembedding_t_e_kernel(tc, x, w1, b1, w2_words, w2_sca
             if SPREAD_UNITS <= r + 7 < SPREAD_UNITS + FEATURES:
                 fetch(feature(r + 7))
             if 0 <= r + 2 < UNITS:
+                affine_on_scalar(r + 2)
                 affine(r + 2)
             if 0 <= r - 1:
                 bias_and_store(r - 1)

@@ -20,6 +20,7 @@ UNIT_COLS = UNIT_TILES * P
 UNITS = (BATCH_TILES // UNIT_TILES) * FEATURES
 PARK_ROW = BATCH_TILES - FEATURES
 SPREAD_UNITS = 4
+PLANE_COLS = 640
 BANK_TILES = 2
 RUN = 4
 GPSIMD_COLS = 224
@@ -40,7 +41,7 @@ def tile_densefeaturenumericembedding_t_e_kernel(tc, x, w1, b1, w2_words, w2_sca
         stack.enter_context(tc.manual_schedule())
         const = stack.enter_context(tc.tile_pool(name="const", bufs=1))
         x_pool = stack.enter_context(tc.tile_pool(name="x_pool", bufs=3))
-        z_pool = stack.enter_context(tc.tile_pool(name="z_pool", bufs=3))
+        z_pool = stack.enter_context(tc.tile_pool(name="z_pool", bufs=4))
         h_pool = stack.enter_context(tc.tile_pool(name="h_pool", bufs=3))
         q_pool = stack.enter_context(tc.tile_pool(name="q_pool", bufs=2))
         o_pool = stack.enter_context(tc.tile_pool(name="o_pool", bufs=4))
@@ -135,8 +136,8 @@ def tile_densefeaturenumericembedding_t_e_kernel(tc, x, w1, b1, w2_words, w2_sca
                 return
             s = feature(u) * PACK + PACK - 1
             nc.scalar.activation(
-                out=z[:, PACK - 1, :SCALAR_COLS],
-                in_=x_of(u)[:, :SCALAR_COLS],
+                out=z[:, PACK - 1, :PLANE_COLS],
+                in_=x_of(u)[:, :PLANE_COLS],
                 func=relu,
                 scale=w1_col[:, s : s + 1],
                 bias=b1_col[:, s : s + 1],
@@ -145,7 +146,7 @@ def tile_densefeaturenumericembedding_t_e_kernel(tc, x, w1, b1, w2_words, w2_sca
         def affine(u):
             for t in range(PACK):
                 s = feature(u) * PACK + t
-                first = SCALAR_COLS if t == PACK - 1 and u >= SPREAD_UNITS else 0
+                first = PLANE_COLS if t == PACK - 1 and u >= SPREAD_UNITS else 0
                 nc.vector.tensor_scalar(
                     out=live["z", u][:, t, first:],
                     in0=x_of(u)[:, first:],
@@ -156,12 +157,19 @@ def tile_densefeaturenumericembedding_t_e_kernel(tc, x, w1, b1, w2_words, w2_sca
                 )
 
         def regroup_on_scalar(u):
+            cols = SCALAR_COLS // 2 if u == 0 else SCALAR_COLS
             h = h_pool.tile([P, UNIT_COLS, PACK], BF16, align_bytes=64)
             nc.scalar.activation(
-                out=h[:, :SCALAR_COLS, :].rearrange("p (c i) t -> p c t i", i=RUN),
-                in_=live["z", u][:, :, :SCALAR_COLS].rearrange("p t (c i) -> p c t i", i=RUN),
+                out=h[:, :cols, :].rearrange("p (c i) t -> p c t i", i=RUN),
+                in_=live["z", u][:, :, :cols].rearrange("p t (c i) -> p c t i", i=RUN),
                 func=relu,
             )
+            if u == 0:
+                nc.vector.tensor_scalar_max(
+                    out=h[:, cols:SCALAR_COLS, :],
+                    in0=live["z", u][:, :, cols:SCALAR_COLS].rearrange("p t b -> p b t"),
+                    scalar1=0.0,
+                )
             live["h", u] = h
 
         def regroup_on_gpsimd(u):
@@ -228,8 +236,13 @@ def tile_densefeaturenumericembedding_t_e_kernel(tc, x, w1, b1, w2_words, w2_sca
                 park()
             if SPREAD_UNITS <= r + 7 < SPREAD_UNITS + FEATURES:
                 fetch(feature(r + 7))
+            if r == -3:
+                affine_on_scalar(0)
+                affine_on_scalar(1)
+                affine_on_scalar(2)
+            if 0 <= r + 3 < UNITS and r > -3:
+                affine_on_scalar(r + 3)
             if 0 <= r + 2 < UNITS:
-                affine_on_scalar(r + 2)
                 affine(r + 2)
             if 0 <= r - 1:
                 bias_and_store(r - 1)

@@ -20,10 +20,10 @@ UNIT_COLS = UNIT_TILES * P
 UNITS = (BATCH_TILES // UNIT_TILES) * FEATURES
 PARK_ROW = BATCH_TILES - FEATURES
 SPREAD_UNITS = 4
-PLANE_COLS = 640
+PLANE_COLS = UNIT_COLS
 BANK_TILES = 2
 RUN = 4
-GPSIMD_COLS = 224
+GPSIMD_COLS = 320
 SCALAR_COLS = UNIT_COLS - GPSIMD_COLS
 FLOAT32_MAX = 3.4028234663852886e38
 
@@ -147,6 +147,8 @@ def tile_densefeaturenumericembedding_t_e_kernel(tc, x, w1, b1, w2_words, w2_sca
             for t in range(PACK):
                 s = feature(u) * PACK + t
                 first = PLANE_COLS if t == PACK - 1 and u >= SPREAD_UNITS else 0
+                if first == UNIT_COLS:
+                    continue
                 nc.vector.tensor_scalar(
                     out=live["z", u][:, t, first:],
                     in0=x_of(u)[:, first:],

@@ -15,19 +15,22 @@ P = 128
 PACK = 4
 BATCH, FEATURES, HIDDEN, EMBED = 4096, 8, 512, 256
 BATCH_TILES = BATCH // P
+FLOPS = 2 * BATCH * FEATURES * HIDDEN * EMBED
 UNIT_TILES = 8
 UNIT_COLS = UNIT_TILES * P
 UNITS = (BATCH_TILES // UNIT_TILES) * FEATURES
 PARK_ROW = BATCH_TILES - FEATURES
 SPREAD_UNITS = 4
 PLANE_COLS = UNIT_COLS
+TENSOR_UNITS = FLOPS // 10 // (2 * P * P * UNIT_COLS)
+PIECE_COLS = 448
+ONES_ROW = PARK_ROW - 1
+MATMUL_COLS = 512
 BANK_TILES = 2
 RUN = 4
 GPSIMD_COLS = 320
 SCALAR_COLS = UNIT_COLS - GPSIMD_COLS
 FLOAT32_MAX = 3.4028234663852886e38
-
-FLOPS = 2 * BATCH * FEATURES * HIDDEN * EMBED
 
 
 def tile_densefeaturenumericembedding_t_e_kernel(tc, x, w1, b1, w2_words, w2_scales, b2, out):
@@ -47,6 +50,11 @@ def tile_densefeaturenumericembedding_t_e_kernel(tc, x, w1, b1, w2_words, w2_sca
         o_pool = stack.enter_context(tc.tile_pool(name="o_pool", bufs=4))
         x_banks = stack.enter_context(tc.psum_pool(name="x_banks", bufs=2))
         acc_banks = stack.enter_context(tc.psum_pool(name="acc_banks", bufs=6))
+
+        rows = const.tile([P, HIDDEN], BF16)
+        nc.vector.memset(rows[:], 0.0)
+        ones = const.tile([P, FEATURES * EMBED // P * 2], BF16)
+        nc.vector.memset(ones[:], 1.0)
 
         x_sb = const.tile([P, BATCH_TILES * FEATURES], BF16)
         nc.sync.dma_start(out=x_sb[:], in_=x.rearrange("(n c) f -> n (c f)", c=BATCH_TILES))
@@ -109,6 +117,47 @@ def tile_densefeaturenumericembedding_t_e_kernel(tc, x, w1, b1, w2_words, w2_sca
             row = out[PARK_ROW + f : PARK_ROW + f + 1, :].rearrange("r w -> (r w)")
             nc.sync.dma_start(out=x_feat[:, f, :].bitcast(F32), in_=row.partition_broadcast(P))
 
+        nc.sync.dma_start(out=rows[0:FEATURES, :], in_=w1)
+        nc.sync.dma_start(out=rows[FEATURES : 2 * FEATURES, :], in_=b1)
+        pick = const.tile([P, FEATURES], F32)
+        weights = const.tile([P, FEATURES, P], BF16)
+        x_rows = const.tile([P, BATCH], BF16)
+
+        def on_tensor(u):
+            return SPREAD_UNITS <= u < SPREAD_UNITS + TENSOR_UNITS
+
+        def make_weights():
+            nc.vector.tensor_tensor(out=pick[:], in0=ident[:, :FEATURES], in1=ident[:, FEATURES : 2 * FEATURES], op=add)
+            last = rows[:].rearrange("j (p t) -> j t p", t=PACK)[:, PACK - 1, :]
+            nc.vector.tensor_tensor(
+                out=weights[:],
+                in0=last.unsqueeze(1).to_broadcast([P, FEATURES, P]),
+                in1=pick[:].unsqueeze(2).to_broadcast([P, FEATURES, P]),
+                op=mult,
+            )
+
+        def park_ones():
+            row = out[ONES_ROW : ONES_ROW + 1, :].rearrange("r (p w) -> (r p) w", p=P)
+            nc.sync.dma_start(out=row, in_=ones[:].bitcast(F32))
+
+        def fetch_rows():
+            words = x_rows[:].bitcast(F32)
+            one = out[ONES_ROW : ONES_ROW + 1, :].rearrange("r w -> (r w)")
+            nc.sync.dma_start(out=words, in_=one.partition_broadcast(P))
+            nc.sync.dma_start(out=words[0:FEATURES, :], in_=out[PARK_ROW : PARK_ROW + FEATURES, :])
+
+        def plane_on_tensor(u):
+            x_bank = x_banks.tile([P, UNIT_COLS], BF16)
+            for first in range(0, UNIT_COLS, MATMUL_COLS):
+                nc.tensor.matmul(
+                    out=x_bank[:, first : first + MATMUL_COLS],
+                    lhsT=weights[:, feature(u), :],
+                    rhs=x_rows[:, first_tile(u) * P + first : first_tile(u) * P + first + MATMUL_COLS],
+                    start=True,
+                    stop=True,
+                )
+            live["plane", u] = x_bank
+
         def x_of(u):
             if u < SPREAD_UNITS:
                 return live["x_all", u][:]
@@ -135,18 +184,31 @@ def tile_densefeaturenumericembedding_t_e_kernel(tc, x, w1, b1, w2_words, w2_sca
             if u < SPREAD_UNITS:
                 return
             s = feature(u) * PACK + PACK - 1
-            nc.scalar.activation(
-                out=z[:, PACK - 1, :PLANE_COLS],
-                in_=x_of(u)[:, :PLANE_COLS],
-                func=relu,
-                scale=w1_col[:, s : s + 1],
-                bias=b1_col[:, s : s + 1],
-            )
+            if on_tensor(u):
+                nc.scalar.copy(out=z[:, PACK - 1, :], in_=live["plane", u][:])
+            else:
+                nc.scalar.activation(
+                    out=z[:, PACK - 1, :PLANE_COLS],
+                    in_=x_of(u)[:, :PLANE_COLS],
+                    func=relu,
+                    scale=w1_col[:, s : s + 1],
+                    bias=b1_col[:, s : s + 1],
+                )
+            if on_tensor(u):
+                nc.scalar.activation(
+                    out=z[:, PACK - 2, :PIECE_COLS],
+                    in_=x_of(u)[:, :PIECE_COLS],
+                    func=relu,
+                    scale=w1_col[:, s - 1 : s],
+                    bias=b1_col[:, s - 1 : s],
+                )
 
         def affine(u):
             for t in range(PACK):
                 s = feature(u) * PACK + t
                 first = PLANE_COLS if t == PACK - 1 and u >= SPREAD_UNITS else 0
+                if t == PACK - 2 and on_tensor(u):
+                    first = PIECE_COLS
                 if first == UNIT_COLS:
                     continue
                 nc.vector.tensor_scalar(
@@ -226,6 +288,8 @@ def tile_densefeaturenumericembedding_t_e_kernel(tc, x, w1, b1, w2_words, w2_sca
                 spread_on_tensor(r + 3)
             if r == -3:
                 turn_on_tensor()
+            if 0 <= r + 3 < UNITS and on_tensor(r + 3):
+                plane_on_tensor(r + 3)
             if 0 <= r < UNITS:
                 quantise(r)
                 multiply(r)
@@ -236,6 +300,9 @@ def tile_densefeaturenumericembedding_t_e_kernel(tc, x, w1, b1, w2_words, w2_sca
                 spread_copy(r + 3)
             if r == -3:
                 park()
+                park_ones()
+            if r == -2:
+                fetch_rows()
             if SPREAD_UNITS <= r + 7 < SPREAD_UNITS + FEATURES:
                 fetch(feature(r + 7))
             if r == -3:
@@ -246,5 +313,7 @@ def tile_densefeaturenumericembedding_t_e_kernel(tc, x, w1, b1, w2_words, w2_sca
                 affine_on_scalar(r + 3)
             if 0 <= r + 2 < UNITS:
                 affine(r + 2)
+            if r == -1:
+                make_weights()
             if 0 <= r - 1:
                 bias_and_store(r - 1)

@@ -21,15 +21,11 @@ UNIT_COLS = UNIT_TILES * P
 UNITS = (BATCH_TILES // UNIT_TILES) * FEATURES
 PARK_ROW = BATCH_TILES - FEATURES
 SPREAD_UNITS = 4
-PLANE_COLS = UNIT_COLS
-TENSOR_UNITS = FLOPS // 10 // (2 * P * P * UNIT_COLS)
-PIECE_COLS = 448
+DIRECT_COLS = 224
 ONES_ROW = PARK_ROW - 1
-MATMUL_COLS = 512
 BANK_TILES = 2
 RUN = 4
 GPSIMD_COLS = 320
-SCALAR_COLS = UNIT_COLS - GPSIMD_COLS
 FLOAT32_MAX = 3.4028234663852886e38
 
 
@@ -120,21 +116,19 @@ def tile_densefeaturenumericembedding_t_e_kernel(tc, x, w1, b1, w2_words, w2_sca
         nc.sync.dma_start(out=rows[0:FEATURES, :], in_=w1)
         nc.sync.dma_start(out=rows[FEATURES : 2 * FEATURES, :], in_=b1)
         pick = const.tile([P, FEATURES], F32)
-        weights = const.tile([P, FEATURES, P], BF16)
+        weights = const.tile([P, FEATURES, HIDDEN], BF16)
         x_rows = const.tile([P, BATCH], BF16)
 
-        def on_tensor(u):
-            return SPREAD_UNITS <= u < SPREAD_UNITS + TENSOR_UNITS
+        def affine_cols(u):
+            return UNIT_COLS if u < SPREAD_UNITS else UNIT_COLS - DIRECT_COLS
+
+        def scalar_cols(u):
+            return affine_cols(u) - GPSIMD_COLS
 
         def make_weights():
             nc.vector.tensor_tensor(out=pick[:], in0=ident[:, :FEATURES], in1=ident[:, FEATURES : 2 * FEATURES], op=add)
-            last = rows[:].rearrange("j (p t) -> j t p", t=PACK)[:, PACK - 1, :]
-            nc.vector.tensor_tensor(
-                out=weights[:],
-                in0=last.unsqueeze(1).to_broadcast([P, FEATURES, P]),
-                in1=pick[:].unsqueeze(2).to_broadcast([P, FEATURES, P]),
-                op=mult,
-            )
+            for f in range(FEATURES):
+                nc.vector.tensor_scalar_mul(out=weights[:, f, :], in0=rows[:], scalar1=pick[:, f : f + 1])
 
         def park_ones():
             row = out[ONES_ROW : ONES_ROW + 1, :].rearrange("r (p w) -> (r p) w", p=P)
@@ -146,17 +140,19 @@ def tile_densefeaturenumericembedding_t_e_kernel(tc, x, w1, b1, w2_words, w2_sca
             nc.sync.dma_start(out=words, in_=one.partition_broadcast(P))
             nc.sync.dma_start(out=words[0:FEATURES, :], in_=out[PARK_ROW : PARK_ROW + FEATURES, :])
 
-        def plane_on_tensor(u):
-            x_bank = x_banks.tile([P, UNIT_COLS], BF16)
-            for first in range(0, UNIT_COLS, MATMUL_COLS):
+        def direct_on_tensor(u):
+            x_bank = x_banks.tile([P, PACK, UNIT_COLS // PACK], BF16)
+            first = first_tile(u) * P + affine_cols(u)
+            by_t = weights[:, feature(u), :].rearrange("j (p t) -> j t p", t=PACK)
+            for t in range(PACK):
                 nc.tensor.matmul(
-                    out=x_bank[:, first : first + MATMUL_COLS],
-                    lhsT=weights[:, feature(u), :],
-                    rhs=x_rows[:, first_tile(u) * P + first : first_tile(u) * P + first + MATMUL_COLS],
+                    out=x_bank[:, t, :DIRECT_COLS],
+                    lhsT=by_t[:, t, :],
+                    rhs=x_rows[:, first : first + DIRECT_COLS],
                     start=True,
                     stop=True,
                 )
-            live["plane", u] = x_bank
+            live["z_bank", u] = x_bank
 
         def x_of(u):
             if u < SPREAD_UNITS:
@@ -184,36 +180,24 @@ def tile_densefeaturenumericembedding_t_e_kernel(tc, x, w1, b1, w2_words, w2_sca
             if u < SPREAD_UNITS:
                 return
             s = feature(u) * PACK + PACK - 1
-            if on_tensor(u):
-                nc.scalar.copy(out=z[:, PACK - 1, :], in_=live["plane", u][:])
-            else:
-                nc.scalar.activation(
-                    out=z[:, PACK - 1, :PLANE_COLS],
-                    in_=x_of(u)[:, :PLANE_COLS],
-                    func=relu,
-                    scale=w1_col[:, s : s + 1],
-                    bias=b1_col[:, s : s + 1],
-                )
-            if on_tensor(u):
-                nc.scalar.activation(
-                    out=z[:, PACK - 2, :PIECE_COLS],
-                    in_=x_of(u)[:, :PIECE_COLS],
-                    func=relu,
-                    scale=w1_col[:, s - 1 : s],
-                    bias=b1_col[:, s - 1 : s],
-                )
+            cols = affine_cols(u)
+            nc.scalar.activation(
+                out=z[:, PACK - 1, :cols],
+                in_=x_of(u)[:, :cols],
+                func=relu,
+                scale=w1_col[:, s : s + 1],
+                bias=b1_col[:, s : s + 1],
+            )
 
         def affine(u):
             for t in range(PACK):
                 s = feature(u) * PACK + t
-                first = PLANE_COLS if t == PACK - 1 and u >= SPREAD_UNITS else 0
-                if t == PACK - 2 and on_tensor(u):
-                    first = PIECE_COLS
-                if first == UNIT_COLS:
+                if t == PACK - 1 and u >= SPREAD_UNITS:
                     continue
+                cols = affine_cols(u)
                 nc.vector.tensor_scalar(
-                    out=live["z", u][:, t, first:],
-                    in0=x_of(u)[:, first:],
+                    out=live["z", u][:, t, :cols],
+                    in0=x_of(u)[:, :cols],
                     scalar1=w1_col[:, s : s + 1],
                     scalar2=b1_col[:, s : s + 1],
                     op0=mult,
@@ -221,8 +205,15 @@ def tile_densefeaturenumericembedding_t_e_kernel(tc, x, w1, b1, w2_words, w2_sca
                 )
 
         def regroup_on_scalar(u):
-            cols = SCALAR_COLS // 2 if u == 0 else SCALAR_COLS
+            s_cols = scalar_cols(u)
+            cols = s_cols // 2 if u == 0 else s_cols
             h = h_pool.tile([P, UNIT_COLS, PACK], BF16, align_bytes=64)
+            if u >= SPREAD_UNITS:
+                nc.scalar.activation(
+                    out=h[:, affine_cols(u) :, :].rearrange("p (c i) t -> p c t i", i=RUN),
+                    in_=live["z_bank", u][:, :, :DIRECT_COLS].rearrange("p t (c i) -> p c t i", i=RUN),
+                    func=relu,
+                )
             nc.scalar.activation(
                 out=h[:, :cols, :].rearrange("p (c i) t -> p c t i", i=RUN),
                 in_=live["z", u][:, :, :cols].rearrange("p t (c i) -> p c t i", i=RUN),
@@ -230,16 +221,16 @@ def tile_densefeaturenumericembedding_t_e_kernel(tc, x, w1, b1, w2_words, w2_sca
             )
             if u == 0:
                 nc.vector.tensor_scalar_max(
-                    out=h[:, cols:SCALAR_COLS, :],
-                    in0=live["z", u][:, :, cols:SCALAR_COLS].rearrange("p t b -> p b t"),
+                    out=h[:, cols:s_cols, :],
+                    in0=live["z", u][:, :, cols:s_cols].rearrange("p t b -> p b t"),
                     scalar1=0.0,
                 )
             live["h", u] = h
 
         def regroup_on_gpsimd(u):
             nc.gpsimd.tensor_scalar(
-                out=live["h", u][:, SCALAR_COLS:, :],
-                in0=live["z", u][:, :, SCALAR_COLS:].rearrange("p t b -> p b t"),
+                out=live["h", u][:, scalar_cols(u) : affine_cols(u), :],
+                in0=live["z", u][:, :, scalar_cols(u) : affine_cols(u)].rearrange("p t b -> p b t"),
                 scalar1=FLOAT32_MAX,
                 scalar2=0.0,
                 op0=mybir.AluOpType.min,
@@ -288,11 +279,11 @@ def tile_densefeaturenumericembedding_t_e_kernel(tc, x, w1, b1, w2_words, w2_sca
                 spread_on_tensor(r + 3)
             if r == -3:
                 turn_on_tensor()
-            if 0 <= r + 3 < UNITS and on_tensor(r + 3):
-                plane_on_tensor(r + 3)
             if 0 <= r < UNITS:
                 quantise(r)
                 multiply(r)
+            if SPREAD_UNITS <= r + 2 < UNITS:
+                direct_on_tensor(r + 2)
             if 0 <= r + 1 < UNITS:
                 regroup_on_scalar(r + 1)
                 regroup_on_gpsimd(r + 1)

@@ -23,6 +23,7 @@ PARK_ROW = BATCH_TILES - FEATURES
 SPREAD_UNITS = 4
 DIRECT_COLS = 224
 ONES_ROW = PARK_ROW - 1
+SPLIT_UNITS = 2
 BANK_TILES = 2
 RUN = 4
 GPSIMD_COLS = 320
@@ -267,12 +268,22 @@ def tile_densefeaturenumericembedding_t_e_kernel(tc, x, w1, b1, w2_words, w2_sca
             f = feature(u)
             o = o_pool.tile([P, UNIT_TILES, EMBED], F32)
             b2_f = b2_all[:, f * EMBED : (f + 1) * EMBED].unsqueeze(1).to_broadcast([P, BANK_TILES, EMBED])
-            for k in range(UNIT_TILES // BANK_TILES):
-                nc.vector.tensor_tensor(
-                    out=o[:, k * BANK_TILES : (k + 1) * BANK_TILES, :], in0=live["acc", u, k][:], in1=b2_f, op=add
-                )
             c0 = first_tile(u)
-            nc.sync.dma_start(out=out_rows[:, c0 : c0 + UNIT_TILES, f * EMBED : (f + 1) * EMBED], in_=o[:])
+            split = u >= UNITS - SPLIT_UNITS
+            banks = list(range(0, UNIT_TILES, BANK_TILES))
+            if not split:
+                banks = banks[-1:] + banks[:-1]
+            for first in banks:
+                after = first + BANK_TILES
+                nc.vector.tensor_tensor(
+                    out=o[:, first:after, :], in0=live["acc", u, first // BANK_TILES][:], in1=b2_f, op=add
+                )
+                if split:
+                    nc.sync.dma_start(
+                        out=out_rows[:, c0 + first : c0 + after, f * EMBED : (f + 1) * EMBED], in_=o[:, first:after, :]
+                    )
+            if not split:
+                nc.sync.dma_start(out=out_rows[:, c0 : c0 + UNIT_TILES, f * EMBED : (f + 1) * EMBED], in_=o[:])
 
         for r in range(-3, UNITS + 1):
             if 0 <= r + 3 < SPREAD_UNITS:

@@ -21,7 +21,8 @@ UNIT_COLS = UNIT_TILES * P
 UNITS = (BATCH_TILES // UNIT_TILES) * FEATURES
 PARK_ROW = BATCH_TILES - FEATURES
 SPREAD_UNITS = 4
-DIRECT_COLS = 224
+DIRECT_UNIT = 8
+DIRECT_COLS = 256
 ONES_ROW = PARK_ROW - 1
 SPLIT_UNITS = 2
 BANK_TILES = 2
@@ -59,6 +60,8 @@ def tile_densefeaturenumericembedding_t_e_kernel(tc, x, w1, b1, w2_words, w2_sca
         nc.sync.dma_start(out=w1_bf[:], in_=w1.rearrange("f (p t) -> p f t", t=PACK))
         b1_bf = const.tile([P, FEATURES, PACK], BF16)
         nc.sync.dma_start(out=b1_bf[:], in_=b1.rearrange("f (p t) -> p f t", t=PACK))
+        nc.sync.dma_start(out=rows[0:FEATURES, :], in_=w1)
+        nc.sync.dma_start(out=rows[FEATURES : 2 * FEATURES, :], in_=b1)
         w2_codes = const.tile([P, FEATURES, 2 * EMBED], U8, align_bytes=64)
         nc.sync.dma_start(out=w2_codes[:].bitcast(I32), in_=w2_words.bitcast(I32).rearrange("g p n -> p g n"))
         w2_planes = const.tile([P, FEATURES, EMBED], U8, align_bytes=64)
@@ -110,18 +113,18 @@ def tile_densefeaturenumericembedding_t_e_kernel(tc, x, w1, b1, w2_words, w2_sca
                     out=pieces[half * P : (half + 1) * P, :], in_=x_turned[:, half * P : (half + 1) * P].bitcast(F32)
                 )
 
-        def fetch(f):
-            row = out[PARK_ROW + f : PARK_ROW + f + 1, :].rearrange("r w -> (r w)")
-            nc.sync.dma_start(out=x_feat[:, f, :].bitcast(F32), in_=row.partition_broadcast(P))
+        def fetch(u, count):
+            row = out[PARK_ROW + feature(u) : PARK_ROW + feature(u) + 1, :].rearrange("r w -> (r w)")
+            first = first_tile(u) * P
+            words = slice(first // 2, (first + count * UNIT_COLS) // 2)
+            nc.sync.dma_start(out=x_feat[:, feature(u), :].bitcast(F32)[:, words], in_=row[words].partition_broadcast(P))
 
-        nc.sync.dma_start(out=rows[0:FEATURES, :], in_=w1)
-        nc.sync.dma_start(out=rows[FEATURES : 2 * FEATURES, :], in_=b1)
         pick = const.tile([P, FEATURES], F32)
         weights = const.tile([P, FEATURES, HIDDEN], BF16)
         x_rows = const.tile([P, BATCH], BF16)
 
         def affine_cols(u):
-            return UNIT_COLS if u < SPREAD_UNITS else UNIT_COLS - DIRECT_COLS
+            return UNIT_COLS if u < DIRECT_UNIT else UNIT_COLS - DIRECT_COLS
 
         def scalar_cols(u):
             return affine_cols(u) - GPSIMD_COLS
@@ -209,7 +212,7 @@ def tile_densefeaturenumericembedding_t_e_kernel(tc, x, w1, b1, w2_words, w2_sca
             s_cols = scalar_cols(u)
             cols = s_cols // 2 if u == 0 else s_cols
             h = h_pool.tile([P, UNIT_COLS, PACK], BF16, align_bytes=64)
-            if u >= SPREAD_UNITS:
+            if u >= DIRECT_UNIT:
                 nc.scalar.activation(
                     out=h[:, affine_cols(u) :, :].rearrange("p (c i) t -> p c t i", i=RUN),
                     in_=live["z_bank", u][:, :, :DIRECT_COLS].rearrange("p t (c i) -> p c t i", i=RUN),
@@ -293,7 +296,7 @@ def tile_densefeaturenumericembedding_t_e_kernel(tc, x, w1, b1, w2_words, w2_sca
             if 0 <= r < UNITS:
                 quantise(r)
                 multiply(r)
-            if SPREAD_UNITS <= r + 2 < UNITS:
+            if DIRECT_UNIT <= r + 2 < UNITS:
                 direct_on_tensor(r + 2)
             if 0 <= r + 1 < UNITS:
                 regroup_on_scalar(r + 1)
@@ -302,11 +305,14 @@ def tile_densefeaturenumericembedding_t_e_kernel(tc, x, w1, b1, w2_words, w2_sca
                 spread_copy(r + 3)
             if r == -3:
                 park()
+            if r == 0:
                 park_ones()
-            if r == -2:
+            if SPREAD_UNITS <= r + 7 < 2 * FEATURES:
+                fetch(r + 7, 1)
+            if 2 * FEATURES <= r + 7 < 3 * FEATURES:
+                fetch(r + 7, 2)
+            if r == 3:
                 fetch_rows()
-            if SPREAD_UNITS <= r + 7 < SPREAD_UNITS + FEATURES:
-                fetch(feature(r + 7))
             if r == -3:
                 affine_on_scalar(0)
                 affine_on_scalar(1)

from contextlib import ExitStack

import concourse.mybir as mybir
from concourse.masks import make_identity

BF16 = mybir.dt.bfloat16
F32 = mybir.dt.float32
I32 = mybir.dt.int32
U32 = mybir.dt.uint32
U8 = mybir.dt.uint8
FP8X4 = mybir.dt.float8_e4m3fn_x4
FP4X4 = mybir.dt.float4_e2m1fn_x4

P = 128
PACK = 4
BATCH, FEATURES, HIDDEN, EMBED = 4096, 8, 512, 256
BATCH_TILES = BATCH // P
FLOPS = 2 * BATCH * FEATURES * HIDDEN * EMBED
UNIT_TILES = 8
UNIT_COLS = UNIT_TILES * P
UNITS = (BATCH_TILES // UNIT_TILES) * FEATURES
PARK_ROW = BATCH_TILES - FEATURES
SPREAD_UNITS = 4
DIRECT_UNIT = 8
DIRECT_COLS = 256
ONES_ROW = PARK_ROW - 1
SPLIT_UNITS = 2
BANK_TILES = 2
RUN = 4
GPSIMD_COLS = 320
FLOAT32_MAX = 3.4028234663852886e38


def tile_densefeaturenumericembedding_t_e_kernel(tc, x, w1, b1, w2_words, w2_scales, b2, out):
    nc = tc.nc
    relu = mybir.ActivationFunctionType.Relu
    mult = mybir.AluOpType.mult
    add = mybir.AluOpType.add
    out_rows = out.rearrange("(n c) w -> n c w", c=BATCH_TILES)

    with ExitStack() as stack:
        stack.enter_context(tc.manual_schedule())
        const = stack.enter_context(tc.tile_pool(name="const", bufs=1))
        x_pool = stack.enter_context(tc.tile_pool(name="x_pool", bufs=3))
        z_pool = stack.enter_context(tc.tile_pool(name="z_pool", bufs=4))
        h_pool = stack.enter_context(tc.tile_pool(name="h_pool", bufs=3))
        q_pool = stack.enter_context(tc.tile_pool(name="q_pool", bufs=2))
        o_pool = stack.enter_context(tc.tile_pool(name="o_pool", bufs=4))
        x_banks = stack.enter_context(tc.psum_pool(name="x_banks", bufs=2))
        acc_banks = stack.enter_context(tc.psum_pool(name="acc_banks", bufs=6))

        rows = const.tile([P, HIDDEN], BF16)
        nc.vector.memset(rows[:], 0.0)
        ones = const.tile([P, FEATURES * EMBED // P * 2], BF16)
        nc.vector.memset(ones[:], 1.0)

        x_sb = const.tile([P, BATCH_TILES * FEATURES], BF16)
        nc.sync.dma_start(out=x_sb[:], in_=x.rearrange("(n c) f -> n (c f)", c=BATCH_TILES))
        w1_bf = const.tile([P, FEATURES, PACK], BF16)
        nc.sync.dma_start(out=w1_bf[:], in_=w1.rearrange("f (p t) -> p f t", t=PACK))
        b1_bf = const.tile([P, FEATURES, PACK], BF16)
        nc.sync.dma_start(out=b1_bf[:], in_=b1.rearrange("f (p t) -> p f t", t=PACK))
        nc.sync.dma_start(out=rows[0:FEATURES, :], in_=w1)
        nc.sync.dma_start(out=rows[FEATURES : 2 * FEATURES, :], in_=b1)
        w2_codes = const.tile([P, FEATURES, 2 * EMBED], U8, align_bytes=64)
        nc.sync.dma_start(out=w2_codes[:].bitcast(I32), in_=w2_words.bitcast(I32).rearrange("g p n -> p g n"))
        w2_planes = const.tile([P, FEATURES, EMBED], U8, align_bytes=64)
        nc.vector.memset(w2_planes[:].rearrange("p g n -> p (g n)").bitcast(I32), 0)
        for quad in range(4):
            nc.sync.dma_start(
                out=w2_planes[32 * quad : 32 * quad + 4, :, :].bitcast(I32),
                in_=w2_scales.bitcast(I32)[:, 4 * quad : 4 * quad + 4, :].rearrange("g q n -> q g n"),
            )
        b2_all = const.tile([P, FEATURES * EMBED], BF16)
        nc.sync.dma_start(out=b2_all[:], in_=b2.rearrange("f e -> (f e)").partition_broadcast(P))

        ident = const.tile([P, P], BF16)
        make_identity(nc, ident[:])
        w1_col = const.tile([P, FEATURES * PACK], F32)
        nc.vector.tensor_copy(out=w1_col[:], in_=w1_bf[:].rearrange("p f t -> p (f t)"))
        b1_col = const.tile([P, FEATURES * PACK], F32)
        nc.vector.tensor_copy(out=b1_col[:], in_=b1_bf[:].rearrange("p f t -> p (f t)"))

        live = {}

        def first_tile(u):
            return (u // FEATURES) * UNIT_TILES

        def feature(u):
            return u % FEATURES

        x_by_feature = const.tile([P, FEATURES * BATCH_TILES], BF16)
        nc.gpsimd.tensor_copy(
            out=x_by_feature[:].rearrange("n (f c) -> n f c", f=FEATURES),
            in_=x_sb[:].rearrange("n (c f) -> n f c", f=FEATURES),
        )
        x_turned = const.tile([P, 2 * P], BF16)
        x_feat = const.tile([P, FEATURES, BATCH], BF16)

        def turn_on_tensor():
            x_bank = x_banks.tile([P, UNIT_COLS], BF16)
            for half in range(2):
                nc.tensor.transpose(
                    x_bank[:, half * P : (half + 1) * P], x_by_feature[:, half * P : (half + 1) * P], ident[:]
                )
            live["turned"] = x_bank

        def park():
            nc.scalar.copy(out=x_turned[:], in_=live["turned"][:, : 2 * P])
            pieces = out[PARK_ROW : PARK_ROW + FEATURES, :].rearrange("f (c w) -> (f c) w", c=BATCH_TILES)
            for half in range(2):
                nc.sync.dma_start(
                    out=pieces[half * P : (half + 1) * P, :], in_=x_turned[:, half * P : (half + 1) * P].bitcast(F32)
                )

        def fetch(u, count):
            row = out[PARK_ROW + feature(u) : PARK_ROW + feature(u) + 1, :].rearrange("r w -> (r w)")
            first = first_tile(u) * P
            words = slice(first // 2, (first + count * UNIT_COLS) // 2)
            nc.sync.dma_start(out=x_feat[:, feature(u), :].bitcast(F32)[:, words], in_=row[words].partition_broadcast(P))

        pick = const.tile([P, FEATURES], F32)
        weights = const.tile([P, FEATURES, HIDDEN], BF16)
        x_rows = const.tile([P, BATCH], BF16)

        def affine_cols(u):
            return UNIT_COLS if u < DIRECT_UNIT else UNIT_COLS - DIRECT_COLS

        def scalar_cols(u):
            return affine_cols(u) - GPSIMD_COLS

        def make_weights():
            nc.vector.tensor_tensor(out=pick[:], in0=ident[:, :FEATURES], in1=ident[:, FEATURES : 2 * FEATURES], op=add)
            for f in range(FEATURES):
                nc.vector.tensor_scalar_mul(out=weights[:, f, :], in0=rows[:], scalar1=pick[:, f : f + 1])

        def park_ones():
            row = out[ONES_ROW : ONES_ROW + 1, :].rearrange("r (p w) -> (r p) w", p=P)
            nc.sync.dma_start(out=row, in_=ones[:].bitcast(F32))

        def fetch_rows():
            words = x_rows[:].bitcast(F32)
            one = out[ONES_ROW : ONES_ROW + 1, :].rearrange("r w -> (r w)")
            nc.sync.dma_start(out=words, in_=one.partition_broadcast(P))
            nc.sync.dma_start(out=words[0:FEATURES, :], in_=out[PARK_ROW : PARK_ROW + FEATURES, :])

        def direct_on_tensor(u):
            x_bank = x_banks.tile([P, PACK, UNIT_COLS // PACK], BF16)
            first = first_tile(u) * P + affine_cols(u)
            by_t = weights[:, feature(u), :].rearrange("j (p t) -> j t p", t=PACK)
            for t in range(PACK):
                nc.tensor.matmul(
                    out=x_bank[:, t, :DIRECT_COLS],
                    lhsT=by_t[:, t, :],
                    rhs=x_rows[:, first : first + DIRECT_COLS],
                    start=True,
                    stop=True,
                )
            live["z_bank", u] = x_bank

        def x_of(u):
            if u < SPREAD_UNITS:
                return live["x_all", u][:]
            first = first_tile(u) * P
            return x_feat[:, feature(u), first : first + UNIT_COLS]

        def spread_on_tensor(u):
            x_bank = x_banks.tile([P, UNIT_COLS], BF16)
            for i in range(UNIT_TILES):
                col = (first_tile(u) + i) * FEATURES + feature(u)
                nc.tensor.transpose(
                    x_bank[:, i * P : (i + 1) * P], x_sb[:, col : col + 1].to_broadcast([P, P]), ident[:]
                )
            live["x_bank", u] = x_bank

        def spread_copy(u):
            x_all = x_pool.tile([P, UNIT_COLS], BF16)
            nc.scalar.copy(out=x_all[:], in_=live["x_bank", u][:])
            live["x_all", u] = x_all

        def affine_on_scalar(u):
            z = z_pool.tile([P, PACK, UNIT_COLS], BF16)
            live["z", u] = z
            if u < SPREAD_UNITS:
                return
            s = feature(u) * PACK + PACK - 1
            cols = affine_cols(u)
            nc.scalar.activation(
                out=z[:, PACK - 1, :cols],
                in_=x_of(u)[:, :cols],
                func=relu,
                scale=w1_col[:, s : s + 1],
                bias=b1_col[:, s : s + 1],
            )

        def affine(u):
            for t in range(PACK):
                s = feature(u) * PACK + t
                if t == PACK - 1 and u >= SPREAD_UNITS:
                    continue
                cols = affine_cols(u)
                nc.vector.tensor_scalar(
                    out=live["z", u][:, t, :cols],
                    in0=x_of(u)[:, :cols],
                    scalar1=w1_col[:, s : s + 1],
                    scalar2=b1_col[:, s : s + 1],
                    op0=mult,
                    op1=add,
                )

        def regroup_on_scalar(u):
            s_cols = scalar_cols(u)
            cols = s_cols // 2 if u == 0 else s_cols
            h = h_pool.tile([P, UNIT_COLS, PACK], BF16, align_bytes=64)
            if u >= DIRECT_UNIT:
                nc.scalar.activation(
                    out=h[:, affine_cols(u) :, :].rearrange("p (c i) t -> p c t i", i=RUN),
                    in_=live["z_bank", u][:, :, :DIRECT_COLS].rearrange("p t (c i) -> p c t i", i=RUN),
                    func=relu,
                )
            nc.scalar.activation(
                out=h[:, :cols, :].rearrange("p (c i) t -> p c t i", i=RUN),
                in_=live["z", u][:, :, :cols].rearrange("p t (c i) -> p c t i", i=RUN),
                func=relu,
            )
            if u == 0:
                nc.vector.tensor_scalar_max(
                    out=h[:, cols:s_cols, :],
                    in0=live["z", u][:, :, cols:s_cols].rearrange("p t b -> p b t"),
                    scalar1=0.0,
                )
            live["h", u] = h

        def regroup_on_gpsimd(u):
            nc.gpsimd.tensor_scalar(
                out=live["h", u][:, scalar_cols(u) : affine_cols(u), :],
                in0=live["z", u][:, :, scalar_cols(u) : affine_cols(u)].rearrange("p t b -> p b t"),
                scalar1=FLOAT32_MAX,
                scalar2=0.0,
                op0=mybir.AluOpType.min,
                op1=mybir.AluOpType.max,
            )

        def quantise(u):
            codes = q_pool.tile([P, UNIT_COLS], U32, align_bytes=64)
            scales = q_pool.tile([P, UNIT_COLS], U8, align_bytes=64)
            nc.vector.quantize_mx(
                out=codes[:].bitcast(FP8X4), scales=scales[:], in_=live["h", u][:].rearrange("p b t -> p (b t)")
            )
            live["codes", u] = codes
            live["scales", u] = scales

        def multiply(u):
            f = feature(u)
            for k in range(UNIT_TILES // BANK_TILES):
                acc = acc_banks.tile([P, BANK_TILES, EMBED], F32)
                for s in range(BANK_TILES):
                    cols = slice((k * BANK_TILES + s) * P, (k * BANK_TILES + s + 1) * P)
                    nc.tensor.matmul_mx(
                        out=acc[:, s, :],
                        lhsT=live["codes", u][:, cols].bitcast(FP8X4),
                        lhsT_scale=live["scales", u][:, cols],
                        rhs=w2_codes[:, f, :].bitcast(FP4X4),
                        rhs_scale=w2_planes[:, f, :],
                        start=True,
                        stop=True,
                    )
                live["acc", u, k] = acc

        def bias_and_store(u):
            f = feature(u)
            o = o_pool.tile([P, UNIT_TILES, EMBED], F32)
            b2_f = b2_all[:, f * EMBED : (f + 1) * EMBED].unsqueeze(1).to_broadcast([P, BANK_TILES, EMBED])
            c0 = first_tile(u)
            split = u >= UNITS - SPLIT_UNITS
            banks = list(range(0, UNIT_TILES, BANK_TILES))
            if not split:
                banks = banks[-1:] + banks[:-1]
            for first in banks:
                after = first + BANK_TILES
                nc.vector.tensor_tensor(
                    out=o[:, first:after, :], in0=live["acc", u, first // BANK_TILES][:], in1=b2_f, op=add
                )
                if split:
                    nc.sync.dma_start(
                        out=out_rows[:, c0 + first : c0 + after, f * EMBED : (f + 1) * EMBED], in_=o[:, first:after, :]
                    )
            if not split:
                nc.sync.dma_start(out=out_rows[:, c0 : c0 + UNIT_TILES, f * EMBED : (f + 1) * EMBED], in_=o[:])

        for r in range(-3, UNITS + 1):
            if 0 <= r + 3 < SPREAD_UNITS:
                spread_on_tensor(r + 3)
            if r == -3:
                turn_on_tensor()
            if 0 <= r < UNITS:
                quantise(r)
                multiply(r)
            if DIRECT_UNIT <= r + 2 < UNITS:
                direct_on_tensor(r + 2)
            if 0 <= r + 1 < UNITS:
                regroup_on_scalar(r + 1)
                regroup_on_gpsimd(r + 1)
            if 0 <= r + 3 < SPREAD_UNITS:
                spread_copy(r + 3)
            if r == -3:
                park()
            if r == 0:
                park_ones()
            if SPREAD_UNITS <= r + 7 < 2 * FEATURES:
                fetch(r + 7, 1)
            if 2 * FEATURES <= r + 7 < 3 * FEATURES:
                fetch(r + 7, 2)
            if r == 3:
                fetch_rows()
            if r == -3:
                affine_on_scalar(0)
                affine_on_scalar(1)
                affine_on_scalar(2)
            if 0 <= r + 3 < UNITS and r > -3:
                affine_on_scalar(r + 3)
            if 0 <= r + 2 < UNITS:
                affine(r + 2)
            if r == -1:
                make_weights()
            if 0 <= r - 1:
                bias_and_store(r - 1)
